import numpy as np
import ml_dtypes


def mxq(x, axis, fmt="e4m3"):
    dtype, down = {"e4m3": (ml_dtypes.float8_e4m3fn, 7), "e5m2": (ml_dtypes.float8_e5m2, 14)}[fmt]
    v = np.moveaxis(np.asarray(x, np.float32).astype(ml_dtypes.bfloat16).astype(np.float64), axis, -1)
    blocks = v.reshape(v.shape[:-1] + (-1, 32))
    amax = np.abs(blocks).max(-1, keepdims=True)
    byte = np.maximum(np.where(amax > 0, np.frexp(amax)[1] - 1 + 127, 0) - down, 1)
    scale = np.exp2(byte - 127.0)
    codes = (blocks / scale).astype(np.float32).astype(dtype).astype(np.float64)
    return np.moveaxis((codes * scale).reshape(v.shape), -1, axis)


WIDE = False


def mx_kscale(k):
    if not WIDE:
        return np.ones(k)
    levels = np.array([10, -10, 5, -5, 0])
    if k % 512:
        return np.exp2(np.random.permutation(np.resize(levels, k // 32))).repeat(32)
    a = np.empty((k // 512, 16))
    for p in range(k // 512):
        a[p, :8] = np.random.permutation(np.resize(levels, 8))
        for g in range(8):
            far = levels[np.abs(levels - a[p, g]) >= 10]
            a[p, g + 8] = far[np.random.randint(len(far))]
    return np.exp2(a.ravel()).repeat(32)


BF16 = ml_dtypes.bfloat16


def bf(x):
    return np.asarray(x, np.float32).astype(BF16)


def f64(x):
    return np.asarray(x).astype(np.float64)


B, S, H, NH, NKV, HD = 2, 4096, 512, 2, 1, 128
ROPE_THETA = 10000.0


def rope_tables():
    inv_freq = 1.0 / (ROPE_THETA ** (np.arange(0, HD, 2) / HD))
    pos = np.arange(S)[None, :] + np.random.randint(0, S, (B, 1))
    freqs = pos[:, :, None] * inv_freq[None, None, :]
    emb = np.concatenate([freqs, freqs], axis=-1)
    return np.cos(emb), np.sin(emb)


def rotate_half(x):
    x1, x2 = np.split(x, 2, axis=-1)
    return np.concatenate([-x2, x1], axis=-1)


def setup_inputs():
    s = mx_kscale(H)
    hidden_states = bf(np.random.standard_normal((B, S, H)) * s)
    q_w = bf(np.random.standard_normal((NH * HD, H)) / np.sqrt(H) / s[None, :])
    k_w = bf(np.random.standard_normal((NKV * HD, H)) / np.sqrt(H) / s[None, :])
    v_w = bf(np.random.standard_normal((NKV * HD, H)) / np.sqrt(H) / s[None, :])
    cos, sin = rope_tables()
    return {"hidden_states": hidden_states, "cos": bf(cos), "sin": bf(sin), "q_w": q_w, "k_w": k_w, "v_w": v_w}


def reference(hidden_states, cos, sin, q_w, k_w, v_w):
    b, s, _ = hidden_states.shape
    xq = mxq(f64(hidden_states), 2, "e4m3")
    q = (xq @ mxq(f64(q_w), 1, "e4m3").T).reshape(b, s, NH, HD).transpose(0, 2, 1, 3)
    k = (xq @ mxq(f64(k_w), 1, "e4m3").T).reshape(b, s, NKV, HD).transpose(0, 2, 1, 3)
    v = (xq @ mxq(f64(v_w), 1, "e4m3").T).reshape(b, s, NKV, HD).transpose(0, 2, 1, 3)
    c = f64(cos)[:, None, :, :]
    sn = f64(sin)[:, None, :, :]
    q = q * c + rotate_half(q) * sn
    k = k * c + rotate_half(k) * sn
    return (q, k, v)

@@ -1,0 +1,257 @@
+from contextlib import ExitStack
+
+import concourse.mybir as mybir
+from concourse.masks import make_identity
+
+F32 = mybir.dt.float32
+BF16 = mybir.dt.bfloat16
+U32 = mybir.dt.uint32
+U8 = mybir.dt.uint8
+FP8X4 = mybir.dt.float8_e4m3fn_x4
+ALU = mybir.AluOpType
+
+P = 128
+B, S, H, HD = 2, 4096, 512, 128
+TPB = S // P
+GT = 4
+BT = 8
+NBLK = B * TPB // BT
+GPB = BT // GT
+NG = NBLK * GPB
+XBUFS = 6
+FLOPS = 2 * B * S * H * 512
+
+
+def tile_mistralattention_t_kernel(tc, hidden_states, cos, sin, q_w, k_w, v_w, out_0, out_1, out_2):
+    nc = tc.nc
+    with ExitStack() as ctx:
+        const = ctx.enter_context(tc.tile_pool(name="const", bufs=1))
+        xpool = ctx.enter_context(tc.tile_pool(name="xpool", bufs=XBUFS))
+        cspool = ctx.enter_context(tc.tile_pool(name="cspool", bufs=XBUFS))
+        snpool = ctx.enter_context(tc.tile_pool(name="snpool", bufs=6))
+        gpool = ctx.enter_context(tc.tile_pool(name="gpool", bufs=3))
+        qpool = ctx.enter_context(tc.tile_pool(name="qpool", bufs=3))
+        tpool = ctx.enter_context(tc.tile_pool(name="tpool", bufs=8))
+        ps_t = ctx.enter_context(tc.psum_pool(name="ps_t", bufs=2))
+        ps_y = ctx.enter_context(tc.psum_pool(name="ps_y", bufs=6))
+        ctx.enter_context(tc.manual_schedule())
+
+        ident = const.tile([P, P], F32)
+        make_identity(nc, ident[:])
+
+        w_sb = const.tile([P, 4 * H], BF16)
+        wgrp = const.tile([P, 4 * H], BF16, align_bytes=64)
+        wc = const.tile([P, 4 * P], U32, align_bytes=64)
+        ws = const.tile([P, 4 * P], U8, align_bytes=64)
+
+        xs_blk = {}
+        cs_blk = {}
+        sn_blk = {}
+
+        def new_block(n):
+            xs_blk[n] = xpool.tile([P, BT * H], BF16, name="xb")
+            cs_blk[n] = cspool.tile([P, 2, BT, HD], BF16, name="cs")
+            sn_blk[n] = snpool.tile([P, BT, HD], BF16, name="sn")
+
+        def load_x(n, ta, tb):
+            b, t0 = divmod(n * BT, TPB)
+            xv = hidden_states[b].rearrange("(p t) k -> p t k", t=TPB)
+            nc.sync.dma_start(
+                out=xs_blk[n][:, ta * H : tb * H], in_=xv[:, t0 + ta : t0 + tb, :].rearrange("p t k -> p (t k)")
+            )
+
+        def load_tables(n):
+            b, t0 = divmod(n * BT, TPB)
+            nc.sync.dma_start(out=sn_blk[n][:], in_=sin[b].rearrange("(p t) d -> p t d", t=TPB)[:, t0 : t0 + BT, :])
+            nc.sync.dma_start(
+                out=cs_blk[n][:, 0], in_=cos[b].rearrange("(p t) d -> p t d", t=TPB)[:, t0 : t0 + BT, :]
+            )
+
+        def load_block(n):
+            new_block(n)
+            load_x(n, 0, BT)
+            load_tables(n)
+
+        def swap_sin(n, on_vector):
+            cs, sn = cs_blk[n], sn_blk[n]
+            if on_vector:
+                nc.vector.tensor_copy(out=cs[:, 1, :, 0:64], in_=sn[:, :, 64:128])
+                nc.vector.tensor_scalar_mul(out=cs[:, 1, :, 64:128], in0=sn[:, :, 0:64], scalar1=-1.0)
+            else:
+                nc.scalar.copy(out=cs[:, 1, :, 0:64], in_=sn[:, :, 64:128])
+                nc.scalar.mul(out=cs[:, 1, :, 64:128], in_=sn[:, :, 0:64], mul=-1.0)
+
+        def transpose_pair(src_words, dst_words, on_vector):
+            xt = ps_t.tile([P, 512], F32, name="xt")
+            for j in range(4):
+                a, u = divmod(j, 2)
+                nc.tensor.transpose(
+                    xt[:, j * 128 : (j + 1) * 128], src_words[:, a * 256 + u : (a + 1) * 256 : 2], ident[:]
+                )
+            dst = dst_words.rearrange("p (a r u) -> p a r u", a=2, u=2)
+            src = xt[:].rearrange("p (a u r) -> p a r u", a=2, u=2)
+            if on_vector:
+                nc.vector.tensor_copy(out=dst, in_=src)
+            else:
+                nc.scalar.copy(out=dst, in_=src)
+
+        def quantise(grp, codes, scales, c0, c1):
+            nc.vector.quantize_mx(
+                out=codes[:, c0:c1].bitcast(FP8X4), scales=scales[:, c0:c1], in_=grp[:, 4 * c0 : 4 * c1]
+            )
+
+        grp_of = {}
+        q_of = {}
+
+        def prep_half(g, half):
+            n, gi = divmod(g, GPB)
+            if half == 0:
+                grp_of[g] = gpool.tile([P, GT * H], BF16, name="grp", align_bytes=64)
+            xw = xs_blk[n][:].bitcast(F32)
+            c = gi * GT * 256 + half * 512
+            transpose_pair(xw[:, c : c + 512], grp_of[g][:].bitcast(F32)[:, half * 512 : (half + 1) * 512], False)
+
+        def prep(g):
+            prep_half(g, 0)
+            prep_half(g, 1)
+
+        def new_codes(g):
+            xc = qpool.tile([P, GT * P], U32, name="xc", align_bytes=64)
+            xs = qpool.tile([P, GT * P], U8, name="xs", align_bytes=64)
+            q_of[g] = (xc, xs)
+
+        def quant(g):
+            new_codes(g)
+            quantise(grp_of[g], q_of[g][0], q_of[g][1], 0, GT * P)
+
+        t_blk = {}
+        v_blk = {}
+
+        def combine(eng, g, h0, h1):
+            tt = t_blk[g]
+            res = tt[:, 0, h0:h1, :, :].rearrange("p h t (f j) -> p (h t) f j", f=2)
+            oth = tt[:, 1, h0:h1, :, :].rearrange("p h t (f j) -> p (h t) f j", f=2)
+            eng.tensor_tensor(out=res, in0=res, in1=oth[:, :, ::-1, :], op=ALU.add)
+
+        def store(g, what):
+            b, t0 = divmod(g * GT, TPB)
+            tt, vo = t_blk[g], v_blk[g]
+            if what == "q0" or what == "q1":
+                h = 0 if what == "q0" else 1
+                nc.sync.dma_start(
+                    out=out_0[b, h].rearrange("(p t) d -> p t d", t=TPB)[:, t0 : t0 + GT, :], in_=tt[:, 0, h, :, :]
+                )
+            elif what == "q":
+                nc.sync.dma_start(
+                    out=out_0[b].rearrange("h (p t) d -> p h t d", t=TPB)[:, :, t0 : t0 + GT, :], in_=tt[:, 0, 0:2, :, :]
+                )
+            elif what == "k":
+                nc.sync.dma_start(
+                    out=out_1[b, 0].rearrange("(p t) d -> p t d", t=TPB)[:, t0 : t0 + GT, :], in_=tt[:, 0, 2, :, :]
+                )
+            else:
+                nc.sync.dma_start(out=out_2[b, 0].rearrange("(p t) d -> p t d", t=TPB)[:, t0 : t0 + GT, :], in_=vo[:])
+
+        def passes(g, hb):
+            xc, xs = q_of[g]
+            y = ps_y.tile([P, 512], F32, name="y")
+            for j in range(GT):
+                nc.tensor.matmul_mx(
+                    out=y[:, j * P : (j + 1) * P],
+                    lhsT=xc[:, j * P : (j + 1) * P].bitcast(FP8X4),
+                    lhsT_scale=xs[:, j * P : (j + 1) * P],
+                    rhs=wc[:, hb * P : (hb + 1) * P].bitcast(FP8X4),
+                    rhs_scale=ws[:, hb * P : (hb + 1) * P],
+                    start=True,
+                    stop=True,
+                )
+            return y
+
+        def head(g, hb):
+            n, gi = divmod(g, GPB)
+            if g not in t_blk:
+                t_blk[g] = tpool.tile([P, 2, 3, GT, HD], F32, name="tt")
+                v_blk[g] = tpool.tile([P, GT, HD], F32, name="vo")
+            tt, vo, cs = t_blk[g], v_blk[g], cs_blk[n]
+            t0 = gi * GT
+            y = passes(g, hb)
+            if hb < 3:
+                nc.vector.tensor_tensor(
+                    out=tt[:, :, hb, :, :].rearrange("p r t d -> p r (t d)"),
+                    in0=y[:].unsqueeze(1).to_broadcast([P, 2, 512]),
+                    in1=cs[:, :, t0 : t0 + GT, :].rearrange("p r t d -> p r (t d)"),
+                    op=ALU.mult,
+                )
+            else:
+                nc.scalar.copy(out=vo[:].rearrange("p t d -> p (t d)"), in_=y[:])
+
+        ww = w_sb[:].bitcast(F32)
+        wgw = wgrp[:].bitcast(F32)
+        new_block(0)
+        nc.sync.dma_start(
+            out=w_sb[:, 0 : 2 * H].rearrange("p (a k) -> p a k", a=2), in_=q_w.rearrange("(a p) k -> p a k", p=P)
+        )
+        load_x(0, 0, 2)
+        load_x(0, 2, 4)
+        load_tables(0)
+        nc.sync.dma_start(out=w_sb[:, 2 * H : 3 * H], in_=k_w)
+        nc.sync.dma_start(out=w_sb[:, 3 * H : 4 * H], in_=v_w)
+        load_x(0, 4, 8)
+        new_block(1)
+        load_x(1, 0, 4)
+        load_x(1, 4, 8)
+        load_tables(1)
+        for n in range(2, XBUFS):
+            load_block(n)
+
+        transpose_pair(ww[:, 0:512], wgw[:, 0:512], True)
+        prep_half(0, 0)
+        prep_half(0, 1)
+        transpose_pair(ww[:, 512:1024], wgw[:, 512:1024], False)
+        new_codes(0)
+        quantise(wgrp, wc, ws, 0, 256)
+        quantise(grp_of[0], q_of[0][0], q_of[0][1], 0, 256)
+        swap_sin(0, True)
+        quantise(grp_of[0], q_of[0][0], q_of[0][1], 256, 512)
+
+        for g in range(NG - 1):
+            n, gi = divmod(g, GPB)
+            head(g, 0)
+            if g == 0:
+                quantise(wgrp, wc, ws, 256, 512)
+            head(g, 1)
+            if g == 0:
+                prep(1)
+                quant(1)
+            head(g, 2)
+            head(g, 3)
+            if g + 2 < NG:
+                prep(g + 2)
+                quant(g + 2)
+            if gi == 0 and n + 1 < NBLK:
+                swap_sin(n + 1, False)
+            if g < NG - 2:
+                combine(nc.gpsimd, g, 0, 3)
+                for what in ("v", "q", "k"):
+                    store(g, what)
+            else:
+                store(g, "v")
+                combine(nc.gpsimd, g, 0, 2)
+                store(g, "q")
+                combine(nc.gpsimd, g, 2, 3)
+                store(g, "k")
+            if gi == GPB - 1 and n + XBUFS < NBLK:
+                load_block(n + XBUFS)
+
+        g = NG - 1
+        head(g, 3)
+        store(g, "v")
+        head(g, 0)
+        head(g, 1)
+        head(g, 2)
+        combine(nc.vector, g, 0, 1)
+        store(g, "q0")
+        combine(nc.vector, g, 1, 2)
+        store(g, "q1")
+        combine(nc.vector, g, 2, 3)
+        store(g, "k")

@@ -167,23 +167,28 @@ def tile_mistralattention_t_kernel(tc, hidden_states, cos, sin, q_w, k_w, v_w, o
                 )
             return y
 
-        def head(g, hb):
-            n, gi = divmod(g, GPB)
+        def multiply(g, hb):
             if g not in t_blk:
                 t_blk[g] = tpool.tile([P, 2, 3, GT, HD], F32, name="tt")
                 v_blk[g] = tpool.tile([P, GT, HD], F32, name="vo")
-            tt, vo, cs = t_blk[g], v_blk[g], cs_blk[n]
+            return passes(g, hb)
+
+        def products(g, hb, y, ta, tz):
+            n, gi = divmod(g, GPB)
             t0 = gi * GT
-            y = passes(g, hb)
+            nc.vector.tensor_tensor(
+                out=t_blk[g][:, :, hb, ta:tz, :].rearrange("p r t d -> p r (t d)"),
+                in0=y[:, ta * HD : tz * HD].unsqueeze(1).to_broadcast([P, 2, (tz - ta) * HD]),
+                in1=cs_blk[n][:, :, t0 + ta : t0 + tz, :].rearrange("p r t d -> p r (t d)"),
+                op=ALU.mult,
+            )
+
+        def head(g, hb):
+            y = multiply(g, hb)
             if hb < 3:
-                nc.vector.tensor_tensor(
-                    out=tt[:, :, hb, :, :].rearrange("p r t d -> p r (t d)"),
-                    in0=y[:].unsqueeze(1).to_broadcast([P, 2, 512]),
-                    in1=cs[:, :, t0 : t0 + GT, :].rearrange("p r t d -> p r (t d)"),
-                    op=ALU.mult,
-                )
+                products(g, hb, y, 0, GT)
             else:
-                nc.scalar.copy(out=vo[:].rearrange("p t d -> p (t d)"), in_=y[:])
+                nc.scalar.copy(out=v_blk[g][:].rearrange("p t d -> p (t d)"), in_=y[:])
 
         ww = w_sb[:].bitcast(F32)
         wgw = wgrp[:].bitcast(F32)
@@ -223,11 +228,19 @@ def tile_mistralattention_t_kernel(tc, hidden_states, cos, sin, q_w, k_w, v_w, o
             if g == 0:
                 prep(1)
                 quant(1)
-            head(g, 2)
-            head(g, 3)
-            if g + 2 < NG:
+            if g == 0:
+                y = multiply(g, 2)
                 prep(g + 2)
+                head(g, 3)
+                products(g, 2, y, 0, GT - 1)
                 quant(g + 2)
+                products(g, 2, y, GT - 1, GT)
+            else:
+                head(g, 2)
+                head(g, 3)
+                if g + 2 < NG:
+                    prep(g + 2)
+                    quant(g + 2)
             if gi == 0 and n + 1 < NBLK:
                 swap_sin(n + 1, False)
             if g < NG - 2:

@@ -18,7 +18,10 @@ BT = 8
 NBLK = B * TPB // BT
 GPB = BT // GT
 NG = NBLK * GPB
+PAIRS = 6
 XBUFS = 6
+V_FIRST = 13
+LEAD = 4
 FLOPS = 2 * B * S * H * 512
 
 
@@ -31,7 +34,7 @@ def tile_mistralattention_t_kernel(tc, hidden_states, cos, sin, q_w, k_w, v_w, o
         snpool = ctx.enter_context(tc.tile_pool(name="snpool", bufs=6))
         gpool = ctx.enter_context(tc.tile_pool(name="gpool", bufs=3))
         qpool = ctx.enter_context(tc.tile_pool(name="qpool", bufs=3))
-        tpool = ctx.enter_context(tc.tile_pool(name="tpool", bufs=8))
+        tpool = ctx.enter_context(tc.tile_pool(name="tpool", bufs=6))
         ps_t = ctx.enter_context(tc.psum_pool(name="ps_t", bufs=2))
         ps_y = ctx.enter_context(tc.psum_pool(name="ps_y", bufs=6))
         ctx.enter_context(tc.manual_schedule())
@@ -60,9 +63,12 @@ def tile_mistralattention_t_kernel(tc, hidden_states, cos, sin, q_w, k_w, v_w, o
                 out=xs_blk[n][:, ta * H : tb * H], in_=xv[:, t0 + ta : t0 + tb, :].rearrange("p t k -> p (t k)")
             )
 
-        def load_tables(n):
+        def load_sin(n):
             b, t0 = divmod(n * BT, TPB)
             nc.sync.dma_start(out=sn_blk[n][:], in_=sin[b].rearrange("(p t) d -> p t d", t=TPB)[:, t0 : t0 + BT, :])
+
+        def load_cos(n):
+            b, t0 = divmod(n * BT, TPB)
             nc.sync.dma_start(
                 out=cs_blk[n][:, 0], in_=cos[b].rearrange("(p t) d -> p t d", t=TPB)[:, t0 : t0 + BT, :]
             )
@@ -70,7 +76,8 @@ def tile_mistralattention_t_kernel(tc, hidden_states, cos, sin, q_w, k_w, v_w, o
         def load_block(n):
             new_block(n)
             load_x(n, 0, BT)
-            load_tables(n)
+            load_sin(n)
+            load_cos(n)
 
         def swap_sin(n, on_vector):
             cs, sn = cs_blk[n], sn_blk[n]
@@ -81,8 +88,8 @@ def tile_mistralattention_t_kernel(tc, hidden_states, cos, sin, q_w, k_w, v_w, o
                 nc.scalar.copy(out=cs[:, 1, :, 0:64], in_=sn[:, :, 64:128])
                 nc.scalar.mul(out=cs[:, 1, :, 64:128], in_=sn[:, :, 0:64], mul=-1.0)
 
-        def transpose_pair(src_words, dst_words, on_vector):
-            xt = ps_t.tile([P, 512], F32, name="xt")
+        def transpose_pair(src_words, dst_words, on_vector, early=False):
+            xt = ps_y.tile([P, 512], F32, name="y") if early else ps_t.tile([P, 512], F32, name="xt")
             for j in range(4):
                 a, u = divmod(j, 2)
                 nc.tensor.transpose(
@@ -103,26 +110,32 @@ def tile_mistralattention_t_kernel(tc, hidden_states, cos, sin, q_w, k_w, v_w, o
         grp_of = {}
         q_of = {}
 
+        def chunk(g):
+            return (g - g % 2, 2) if g >= PAIRS else (g, 1)
+
         def prep_half(g, half):
             n, gi = divmod(g, GPB)
-            if half == 0:
-                grp_of[g] = gpool.tile([P, GT * H], BF16, name="grp", align_bytes=64)
+            first, groups = chunk(g)
+            if half == 0 and g == first:
+                grp_of[first] = gpool.tile([P, groups * GT * H], BF16, name="grp", align_bytes=64)
             xw = xs_blk[n][:].bitcast(F32)
             c = gi * GT * 256 + half * 512
-            transpose_pair(xw[:, c : c + 512], grp_of[g][:].bitcast(F32)[:, half * 512 : (half + 1) * 512], False)
+            d = (g - first) * GT * 256 + half * 512
+            transpose_pair(xw[:, c : c + 512], grp_of[first][:].bitcast(F32)[:, d : d + 512], False)
 
         def prep(g):
             prep_half(g, 0)
             prep_half(g, 1)
 
         def new_codes(g):
-            xc = qpool.tile([P, GT * P], U32, name="xc", align_bytes=64)
-            xs = qpool.tile([P, GT * P], U8, name="xs", align_bytes=64)
+            width = chunk(g)[1] * GT * P
+            xc = qpool.tile([P, width], U32, name="xc", align_bytes=64)
+            xs = qpool.tile([P, width], U8, name="xs", align_bytes=64)
             q_of[g] = (xc, xs)
 
         def quant(g):
             new_codes(g)
-            quantise(grp_of[g], q_of[g][0], q_of[g][1], 0, GT * P)
+            quantise(grp_of[g], q_of[g][0], q_of[g][1], 0, chunk(g)[1] * GT * P)
 
         t_blk = {}
         v_blk = {}
@@ -153,13 +166,15 @@ def tile_mistralattention_t_kernel(tc, hidden_states, cos, sin, q_w, k_w, v_w, o
                 nc.sync.dma_start(out=out_2[b, 0].rearrange("(p t) d -> p t d", t=TPB)[:, t0 : t0 + GT, :], in_=vo[:])
 
         def passes(g, hb):
-            xc, xs = q_of[g]
+            first = chunk(g)[0]
+            xc, xs = q_of[first]
             y = ps_y.tile([P, 512], F32, name="y")
             for j in range(GT):
+                c = ((g - first) * GT + j) * P
                 nc.tensor.matmul_mx(
                     out=y[:, j * P : (j + 1) * P],
-                    lhsT=xc[:, j * P : (j + 1) * P].bitcast(FP8X4),
-                    lhsT_scale=xs[:, j * P : (j + 1) * P],
+                    lhsT=xc[:, c : c + P].bitcast(FP8X4),
+                    lhsT_scale=xs[:, c : c + P],
                     rhs=wc[:, hb * P : (hb + 1) * P].bitcast(FP8X4),
                     rhs_scale=ws[:, hb * P : (hb + 1) * P],
                     start=True,
@@ -198,29 +213,44 @@ def tile_mistralattention_t_kernel(tc, hidden_states, cos, sin, q_w, k_w, v_w, o
         )
         load_x(0, 0, 2)
         load_x(0, 2, 4)
-        load_tables(0)
+        load_sin(0)
         nc.sync.dma_start(out=w_sb[:, 2 * H : 3 * H], in_=k_w)
         nc.sync.dma_start(out=w_sb[:, 3 * H : 4 * H], in_=v_w)
+        load_cos(0)
         load_x(0, 4, 8)
         new_block(1)
         load_x(1, 0, 4)
         load_x(1, 4, 8)
-        load_tables(1)
+        load_sin(1)
+        load_cos(1)
         for n in range(2, XBUFS):
             load_block(n)
 
-        transpose_pair(ww[:, 0:512], wgw[:, 0:512], True)
+        transpose_pair(ww[:, 0:512], wgw[:, 0:512], True, early=True)
         prep_half(0, 0)
         prep_half(0, 1)
-        transpose_pair(ww[:, 512:1024], wgw[:, 512:1024], False)
+        transpose_pair(ww[:, 512:1024], wgw[:, 512:1024], False, early=True)
         new_codes(0)
         quantise(wgrp, wc, ws, 0, 256)
         quantise(grp_of[0], q_of[0][0], q_of[0][1], 0, 256)
-        swap_sin(0, True)
+        nc.vector.tensor_copy(out=cs_blk[0][:, 1, :, 0:64], in_=sn_blk[0][:, :, 64:128])
         quantise(grp_of[0], q_of[0][0], q_of[0][1], 256, 512)
+        nc.vector.tensor_scalar_mul(out=cs_blk[0][:, 1, :, 64:128], in0=sn_blk[0][:, :, 0:64], scalar1=-1.0)
+
+        turned = [2]
+
+        def turn_x(g):
+            while turned[-1] < g:
+                turned.append(turned[-1] + 1)
+                prep(turned[-1])
 
         for g in range(NG - 1):
             n, gi = divmod(g, GPB)
+            if g >= V_FIRST:
+                head(g, 3)
+                store(g, "v")
+                store(g - 1, "q")
+                store(g - 1, "k")
             head(g, 0)
             if g == 0:
                 quantise(wgrp, wc, ws, 256, 512)
@@ -237,28 +267,31 @@ def tile_mistralattention_t_kernel(tc, hidden_states, cos, sin, q_w, k_w, v_w, o
                 products(g, 2, y, GT - 1, GT)
             else:
                 head(g, 2)
-                head(g, 3)
-                if g + 2 < NG:
-                    prep(g + 2)
+                if g < V_FIRST:
+                    head(g, 3)
+                turn_x(min(g + min(g + 1, LEAD), NG - 1))
+                if g + 2 < NG and chunk(g + 2)[0] == g + 2:
                     quant(g + 2)
             if gi == 0 and n + 1 < NBLK:
                 swap_sin(n + 1, False)
             if g < NG - 2:
                 combine(nc.gpsimd, g, 0, 3)
+            else:
+                combine(nc.gpsimd, g, 0, 2)
+                combine(nc.gpsimd, g, 2, 3)
+            if g < V_FIRST - 1:
                 for what in ("v", "q", "k"):
                     store(g, what)
-            else:
+            elif g < V_FIRST:
                 store(g, "v")
-                combine(nc.gpsimd, g, 0, 2)
-                store(g, "q")
-                combine(nc.gpsimd, g, 2, 3)
-                store(g, "k")
             if gi == GPB - 1 and n + XBUFS < NBLK:
                 load_block(n + XBUFS)
 
         g = NG - 1
         head(g, 3)
         store(g, "v")
+        store(g - 1, "q")
+        store(g - 1, "k")
         head(g, 0)
         head(g, 1)
         head(g, 2)

@@ -18,6 +18,7 @@ BT = 8
 NBLK = B * TPB // BT
 GPB = BT // GT
 NG = NBLK * GPB
+TURNED = (11, 13,)
 PAIRS = 6
 XBUFS = 6
 V_FIRST = 13
@@ -41,7 +42,13 @@ def tile_mistralattention_t_kernel(tc, hidden_states, cos, sin, q_w, k_w, v_w, o
 
         ident = const.tile([P, P], F32)
         make_identity(nc, ident[:])
+        half = const.tile([P, P], F32)
+        nc.gpsimd.tensor_copy(out=half[:, 0:64], in_=ident[:, 64:128])
+        nc.gpsimd.tensor_copy(out=half[:, 64:128], in_=ident[:, 0:64])
+        ident_bf = const.tile([P, P], BF16)
+        nc.gpsimd.tensor_copy(out=ident_bf[:], in_=ident[:])
 
+        tabs_of, pt_of = {}, {}
         w_sb = const.tile([P, 4 * H], BF16)
         wgrp = const.tile([P, 4 * H], BF16, align_bytes=64)
         wc = const.tile([P, 4 * P], U32, align_bytes=64)
@@ -182,9 +189,64 @@ def tile_mistralattention_t_kernel(tc, hidden_states, cos, sin, q_w, k_w, v_w, o
                 )
             return y
 
-        def multiply(g, hb):
+        def turn_tables(g):
+            n, gi = divmod(g, GPB)
+            tp = ps_t.tile([P, 2 * GT * P], BF16, name="xt")
+            for r in range(2):
+                for t in range(GT):
+                    c = (r * GT + t) * P
+                    nc.tensor.transpose(tp[:, c : c + P], cs_blk[n][:, r, gi * GT + t, :], ident_bf[:])
+            tabs_of[g] = qpool.tile([P, 2, GT * P], BF16, name="tabs", bufs=2)
+            nc.scalar.copy(out=tabs_of[g][:].rearrange("p r c -> p (r c)"), in_=tp[:])
+
+        def turned_head(g, hb):
+            first = chunk(g)[0]
+            xc, xs = q_of[first]
+            c = (g - first) * GT * P
+            y = ps_y.tile([P, GT * P], F32, name="y")
+            nc.tensor.matmul_mx(
+                out=y[:],
+                lhsT=wc[:, hb * P : (hb + 1) * P].bitcast(FP8X4),
+                lhsT_scale=ws[:, hb * P : (hb + 1) * P],
+                rhs=xc[:, c : c + GT * P].bitcast(FP8X4),
+                rhs_scale=xs[:, c : c + GT * P],
+                start=True,
+                stop=True,
+            )
+            pt = tpool.tile([P, 2, GT * P], F32, name="pt", bufs=3)
+            pt_of[g, hb] = pt
+            if g < NG - 1 and hb in (2,):
+                ys = tpool.tile([P, GT * P], F32, name="ys", bufs=1)
+                nc.scalar.copy(out=ys[:], in_=y[:])
+                nc.gpsimd.tensor_tensor(
+                    out=pt[:], in0=ys[:].unsqueeze(1).to_broadcast([P, 2, GT * P]), in1=tabs_of[g][:], op=ALU.mult
+                )
+                return
+            nc.vector.tensor_tensor(
+                out=pt[:], in0=y[:].unsqueeze(1).to_broadcast([P, 2, GT * P]), in1=tabs_of[g][:], op=ALU.mult
+            )
+
+        def turn_back(g, hb):
+            pt = pt_of[g, hb]
             if g not in t_blk:
                 t_blk[g] = tpool.tile([P, 2, 3, GT, HD], F32, name="tt")
+            z = ps_t.tile([P, GT * HD], F32, name="xt")
+            for t in range(GT):
+                for r, perm in enumerate((ident, half)):
+                    nc.tensor.matmul(
+                        z[:, t * HD : (t + 1) * HD],
+                        lhsT=pt[:, r, t * P : (t + 1) * P],
+                        rhs=perm[:],
+                        start=r == 0,
+                        stop=r == 1,
+                        is_transpose=True,
+                    )
+            nc.scalar.copy(out=t_blk[g][:, 0, hb].rearrange("p t d -> p (t d)"), in_=z[:])
+
+        def multiply(g, hb):
+            if g not in v_blk:
+                if g not in t_blk:
+                    t_blk[g] = tpool.tile([P, 2, 3, GT, HD], F32, name="tt")
                 v_blk[g] = tpool.tile([P, GT, HD], F32, name="vo")
             return passes(g, hb)
 
@@ -199,6 +261,9 @@ def tile_mistralattention_t_kernel(tc, hidden_states, cos, sin, q_w, k_w, v_w, o
             )
 
         def head(g, hb):
+            if g in TURNED and hb < 3:
+                turned_head(g, hb)
+                return
             y = multiply(g, hb)
             if hb < 3:
                 products(g, hb, y, 0, GT)
@@ -237,6 +302,15 @@ def tile_mistralattention_t_kernel(tc, hidden_states, cos, sin, q_w, k_w, v_w, o
         quantise(grp_of[0], q_of[0][0], q_of[0][1], 256, 512)
         nc.vector.tensor_scalar_mul(out=cs_blk[0][:, 1, :, 64:128], in0=sn_blk[0][:, :, 0:64], scalar1=-1.0)
 
+        BACKS = {(1,2): 0,(1,3): 1,(2,1): 2}
+
+        def back(g, pos):
+            for d in (1, 2):
+                if g - d in TURNED and (d, pos) in BACKS:
+                    h = BACKS[d, pos]
+                    turn_back(g - d, h)
+                    store(g - d, ("q0", "q1", "k")[h])
+
         turned = [2]
 
         def turn_x(g):
@@ -249,12 +323,15 @@ def tile_mistralattention_t_kernel(tc, hidden_states, cos, sin, q_w, k_w, v_w, o
             if g >= V_FIRST:
                 head(g, 3)
                 store(g, "v")
-                store(g - 1, "q")
-                store(g - 1, "k")
+                if g - 1 not in TURNED:
+                    store(g - 1, "q")
+                    store(g - 1, "k")
             head(g, 0)
             if g == 0:
                 quantise(wgrp, wc, ws, 256, 512)
+            back(g, 0)
             head(g, 1)
+            back(g, 1)
             if g == 0:
                 prep(1)
                 quant(1)
@@ -267,19 +344,27 @@ def tile_mistralattention_t_kernel(tc, hidden_states, cos, sin, q_w, k_w, v_w, o
                 products(g, 2, y, GT - 1, GT)
             else:
                 head(g, 2)
+                back(g, 2)
                 if g < V_FIRST:
                     head(g, 3)
+                back(g, 3)
                 turn_x(min(g + min(g + 1, LEAD), NG - 1))
                 if g + 2 < NG and chunk(g + 2)[0] == g + 2:
                     quant(g + 2)
             if gi == 0 and n + 1 < NBLK:
                 swap_sin(n + 1, False)
-            if g < NG - 2:
+            if g + 2 in TURNED:
+                turn_tables(g + 2)
+            if g == 13:
+                turn_tables(NG - 1)
+            if g in TURNED:
+                pass
+            elif g < NG - 3:
                 combine(nc.gpsimd, g, 0, 3)
             else:
                 combine(nc.gpsimd, g, 0, 2)
                 combine(nc.gpsimd, g, 2, 3)
-            if g < V_FIRST - 1:
+            if g < V_FIRST - 1 and g not in TURNED:
                 for what in ("v", "q", "k"):
                     store(g, what)
             elif g < V_FIRST:
@@ -292,12 +377,13 @@ def tile_mistralattention_t_kernel(tc, hidden_states, cos, sin, q_w, k_w, v_w, o
         store(g, "v")
         store(g - 1, "q")
         store(g - 1, "k")
+        turned_head(g, 2)
         head(g, 0)
         head(g, 1)
-        head(g, 2)
+        back(g, 1)
+        turn_back(g, 2)
+        store(g, "k")
         combine(nc.vector, g, 0, 1)
         store(g, "q0")
         combine(nc.vector, g, 1, 2)
         store(g, "q1")
-        combine(nc.vector, g, 2, 3)
-        store(g, "k")

@@ -18,7 +18,7 @@ BT = 8
 NBLK = B * TPB // BT
 GPB = BT // GT
 NG = NBLK * GPB
-TURNED = (11, 13,)
+TURNED = (11,)
 PAIRS = 6
 XBUFS = 6
 V_FIRST = 13
@@ -35,7 +35,7 @@ def tile_mistralattention_t_kernel(tc, hidden_states, cos, sin, q_w, k_w, v_w, o
         snpool = ctx.enter_context(tc.tile_pool(name="snpool", bufs=6))
         gpool = ctx.enter_context(tc.tile_pool(name="gpool", bufs=3))
         qpool = ctx.enter_context(tc.tile_pool(name="qpool", bufs=3))
-        tpool = ctx.enter_context(tc.tile_pool(name="tpool", bufs=6))
+        tpool = ctx.enter_context(tc.tile_pool(name="tpool", bufs=5))
         ps_t = ctx.enter_context(tc.psum_pool(name="ps_t", bufs=2))
         ps_y = ctx.enter_context(tc.psum_pool(name="ps_y", bufs=6))
         ctx.enter_context(tc.manual_schedule())
@@ -196,7 +196,7 @@ def tile_mistralattention_t_kernel(tc, hidden_states, cos, sin, q_w, k_w, v_w, o
                 for t in range(GT):
                     c = (r * GT + t) * P
                     nc.tensor.transpose(tp[:, c : c + P], cs_blk[n][:, r, gi * GT + t, :], ident_bf[:])
-            tabs_of[g] = qpool.tile([P, 2, GT * P], BF16, name="tabs", bufs=2)
+            tabs_of[g] = qpool.tile([P, 2, GT * P], F32, name="tabs", bufs=2)
             nc.scalar.copy(out=tabs_of[g][:].rearrange("p r c -> p (r c)"), in_=tp[:])
 
         def turned_head(g, hb):
@@ -302,7 +302,7 @@ def tile_mistralattention_t_kernel(tc, hidden_states, cos, sin, q_w, k_w, v_w, o
         quantise(grp_of[0], q_of[0][0], q_of[0][1], 256, 512)
         nc.vector.tensor_scalar_mul(out=cs_blk[0][:, 1, :, 64:128], in0=sn_blk[0][:, :, 0:64], scalar1=-1.0)
 
-        BACKS = {(1,2): 0,(1,3): 1,(2,1): 2}
+        BACKS = {(1,1): 0,(1,2): 1,(2,1): 2}
 
         def back(g, pos):
             for d in (1, 2):

from contextlib import ExitStack

import concourse.mybir as mybir
from concourse.masks import make_identity

F32 = mybir.dt.float32
BF16 = mybir.dt.bfloat16
U32 = mybir.dt.uint32
U8 = mybir.dt.uint8
FP8X4 = mybir.dt.float8_e4m3fn_x4
ALU = mybir.AluOpType

P = 128
B, S, H, HD = 2, 4096, 512, 128
TPB = S // P
GT = 4
BT = 8
NBLK = B * TPB // BT
GPB = BT // GT
NG = NBLK * GPB
TURNED = (11,)
PAIRS = 6
XBUFS = 6
V_FIRST = 13
LEAD = 4
FLOPS = 2 * B * S * H * 512


def tile_mistralattention_t_kernel(tc, hidden_states, cos, sin, q_w, k_w, v_w, out_0, out_1, out_2):
    nc = tc.nc
    with ExitStack() as ctx:
        const = ctx.enter_context(tc.tile_pool(name="const", bufs=1))
        xpool = ctx.enter_context(tc.tile_pool(name="xpool", bufs=XBUFS))
        cspool = ctx.enter_context(tc.tile_pool(name="cspool", bufs=XBUFS))
        snpool = ctx.enter_context(tc.tile_pool(name="snpool", bufs=6))
        gpool = ctx.enter_context(tc.tile_pool(name="gpool", bufs=3))
        qpool = ctx.enter_context(tc.tile_pool(name="qpool", bufs=3))
        tpool = ctx.enter_context(tc.tile_pool(name="tpool", bufs=5))
        ps_t = ctx.enter_context(tc.psum_pool(name="ps_t", bufs=2))
        ps_y = ctx.enter_context(tc.psum_pool(name="ps_y", bufs=6))
        ctx.enter_context(tc.manual_schedule())

        ident = const.tile([P, P], F32)
        make_identity(nc, ident[:])
        half = const.tile([P, P], F32)
        nc.gpsimd.tensor_copy(out=half[:, 0:64], in_=ident[:, 64:128])
        nc.gpsimd.tensor_copy(out=half[:, 64:128], in_=ident[:, 0:64])
        ident_bf = const.tile([P, P], BF16)
        nc.gpsimd.tensor_copy(out=ident_bf[:], in_=ident[:])

        tabs_of, pt_of = {}, {}
        w_sb = const.tile([P, 4 * H], BF16)
        wgrp = const.tile([P, 4 * H], BF16, align_bytes=64)
        wc = const.tile([P, 4 * P], U32, align_bytes=64)
        ws = const.tile([P, 4 * P], U8, align_bytes=64)

        xs_blk = {}
        cs_blk = {}
        sn_blk = {}

        def new_block(n):
            xs_blk[n] = xpool.tile([P, BT * H], BF16, name="xb")
            cs_blk[n] = cspool.tile([P, 2, BT, HD], BF16, name="cs")
            sn_blk[n] = snpool.tile([P, BT, HD], BF16, name="sn")

        def load_x(n, ta, tb):
            b, t0 = divmod(n * BT, TPB)
            xv = hidden_states[b].rearrange("(p t) k -> p t k", t=TPB)
            nc.sync.dma_start(
                out=xs_blk[n][:, ta * H : tb * H], in_=xv[:, t0 + ta : t0 + tb, :].rearrange("p t k -> p (t k)")
            )

        def load_sin(n):
            b, t0 = divmod(n * BT, TPB)
            nc.sync.dma_start(out=sn_blk[n][:], in_=sin[b].rearrange("(p t) d -> p t d", t=TPB)[:, t0 : t0 + BT, :])

        def load_cos(n):
            b, t0 = divmod(n * BT, TPB)
            nc.sync.dma_start(
                out=cs_blk[n][:, 0], in_=cos[b].rearrange("(p t) d -> p t d", t=TPB)[:, t0 : t0 + BT, :]
            )

        def load_block(n):
            new_block(n)
            load_x(n, 0, BT)
            load_sin(n)
            load_cos(n)

        def swap_sin(n, on_vector):
            cs, sn = cs_blk[n], sn_blk[n]
            if on_vector:
                nc.vector.tensor_copy(out=cs[:, 1, :, 0:64], in_=sn[:, :, 64:128])
                nc.vector.tensor_scalar_mul(out=cs[:, 1, :, 64:128], in0=sn[:, :, 0:64], scalar1=-1.0)
            else:
                nc.scalar.copy(out=cs[:, 1, :, 0:64], in_=sn[:, :, 64:128])
                nc.scalar.mul(out=cs[:, 1, :, 64:128], in_=sn[:, :, 0:64], mul=-1.0)

        def transpose_pair(src_words, dst_words, on_vector, early=False):
            xt = ps_y.tile([P, 512], F32, name="y") if early else ps_t.tile([P, 512], F32, name="xt")
            for j in range(4):
                a, u = divmod(j, 2)
                nc.tensor.transpose(
                    xt[:, j * 128 : (j + 1) * 128], src_words[:, a * 256 + u : (a + 1) * 256 : 2], ident[:]
                )
            dst = dst_words.rearrange("p (a r u) -> p a r u", a=2, u=2)
            src = xt[:].rearrange("p (a u r) -> p a r u", a=2, u=2)
            if on_vector:
                nc.vector.tensor_copy(out=dst, in_=src)
            else:
                nc.scalar.copy(out=dst, in_=src)

        def quantise(grp, codes, scales, c0, c1):
            nc.vector.quantize_mx(
                out=codes[:, c0:c1].bitcast(FP8X4), scales=scales[:, c0:c1], in_=grp[:, 4 * c0 : 4 * c1]
            )

        grp_of = {}
        q_of = {}

        def chunk(g):
            return (g - g % 2, 2) if g >= PAIRS else (g, 1)

        def prep_half(g, half):
            n, gi = divmod(g, GPB)
            first, groups = chunk(g)
            if half == 0 and g == first:
                grp_of[first] = gpool.tile([P, groups * GT * H], BF16, name="grp", align_bytes=64)
            xw = xs_blk[n][:].bitcast(F32)
            c = gi * GT * 256 + half * 512
            d = (g - first) * GT * 256 + half * 512
            transpose_pair(xw[:, c : c + 512], grp_of[first][:].bitcast(F32)[:, d : d + 512], False)

        def prep(g):
            prep_half(g, 0)
            prep_half(g, 1)

        def new_codes(g):
            width = chunk(g)[1] * GT * P
            xc = qpool.tile([P, width], U32, name="xc", align_bytes=64)
            xs = qpool.tile([P, width], U8, name="xs", align_bytes=64)
            q_of[g] = (xc, xs)

        def quant(g):
            new_codes(g)
            quantise(grp_of[g], q_of[g][0], q_of[g][1], 0, chunk(g)[1] * GT * P)

        t_blk = {}
        v_blk = {}

        def combine(eng, g, h0, h1):
            tt = t_blk[g]
            res = tt[:, 0, h0:h1, :, :].rearrange("p h t (f j) -> p (h t) f j", f=2)
            oth = tt[:, 1, h0:h1, :, :].rearrange("p h t (f j) -> p (h t) f j", f=2)
            eng.tensor_tensor(out=res, in0=res, in1=oth[:, :, ::-1, :], op=ALU.add)

        def store(g, what):
            b, t0 = divmod(g * GT, TPB)
            tt, vo = t_blk[g], v_blk[g]
            if what == "q0" or what == "q1":
                h = 0 if what == "q0" else 1
                nc.sync.dma_start(
                    out=out_0[b, h].rearrange("(p t) d -> p t d", t=TPB)[:, t0 : t0 + GT, :], in_=tt[:, 0, h, :, :]
                )
            elif what == "q":
                nc.sync.dma_start(
                    out=out_0[b].rearrange("h (p t) d -> p h t d", t=TPB)[:, :, t0 : t0 + GT, :], in_=tt[:, 0, 0:2, :, :]
                )
            elif what == "k":
                nc.sync.dma_start(
                    out=out_1[b, 0].rearrange("(p t) d -> p t d", t=TPB)[:, t0 : t0 + GT, :], in_=tt[:, 0, 2, :, :]
                )
            else:
                nc.sync.dma_start(out=out_2[b, 0].rearrange("(p t) d -> p t d", t=TPB)[:, t0 : t0 + GT, :], in_=vo[:])

        def passes(g, hb):
            first = chunk(g)[0]
            xc, xs = q_of[first]
            y = ps_y.tile([P, 512], F32, name="y")
            for j in range(GT):
                c = ((g - first) * GT + j) * P
                nc.tensor.matmul_mx(
                    out=y[:, j * P : (j + 1) * P],
                    lhsT=xc[:, c : c + P].bitcast(FP8X4),
                    lhsT_scale=xs[:, c : c + P],
                    rhs=wc[:, hb * P : (hb + 1) * P].bitcast(FP8X4),
                    rhs_scale=ws[:, hb * P : (hb + 1) * P],
                    start=True,
                    stop=True,
                )
            return y

        def turn_tables(g):
            n, gi = divmod(g, GPB)
            tp = ps_t.tile([P, 2 * GT * P], BF16, name="xt")
            for r in range(2):
                for t in range(GT):
                    c = (r * GT + t) * P
                    nc.tensor.transpose(tp[:, c : c + P], cs_blk[n][:, r, gi * GT + t, :], ident_bf[:])
            tabs_of[g] = qpool.tile([P, 2, GT * P], F32, name="tabs", bufs=2)
            nc.scalar.copy(out=tabs_of[g][:].rearrange("p r c -> p (r c)"), in_=tp[:])

        def turned_head(g, hb):
            first = chunk(g)[0]
            xc, xs = q_of[first]
            c = (g - first) * GT * P
            y = ps_y.tile([P, GT * P], F32, name="y")
            nc.tensor.matmul_mx(
                out=y[:],
                lhsT=wc[:, hb * P : (hb + 1) * P].bitcast(FP8X4),
                lhsT_scale=ws[:, hb * P : (hb + 1) * P],
                rhs=xc[:, c : c + GT * P].bitcast(FP8X4),
                rhs_scale=xs[:, c : c + GT * P],
                start=True,
                stop=True,
            )
            pt = tpool.tile([P, 2, GT * P], F32, name="pt", bufs=3)
            pt_of[g, hb] = pt
            if g < NG - 1 and hb in (2,):
                ys = tpool.tile([P, GT * P], F32, name="ys", bufs=1)
                nc.scalar.copy(out=ys[:], in_=y[:])
                nc.gpsimd.tensor_tensor(
                    out=pt[:], in0=ys[:].unsqueeze(1).to_broadcast([P, 2, GT * P]), in1=tabs_of[g][:], op=ALU.mult
                )
                return
            nc.vector.tensor_tensor(
                out=pt[:], in0=y[:].unsqueeze(1).to_broadcast([P, 2, GT * P]), in1=tabs_of[g][:], op=ALU.mult
            )

        def turn_back(g, hb):
            pt = pt_of[g, hb]
            if g not in t_blk:
                t_blk[g] = tpool.tile([P, 2, 3, GT, HD], F32, name="tt")
            z = ps_t.tile([P, GT * HD], F32, name="xt")
            for t in range(GT):
                for r, perm in enumerate((ident, half)):
                    nc.tensor.matmul(
                        z[:, t * HD : (t + 1) * HD],
                        lhsT=pt[:, r, t * P : (t + 1) * P],
                        rhs=perm[:],
                        start=r == 0,
                        stop=r == 1,
                        is_transpose=True,
                    )
            nc.scalar.copy(out=t_blk[g][:, 0, hb].rearrange("p t d -> p (t d)"), in_=z[:])

        def multiply(g, hb):
            if g not in v_blk:
                if g not in t_blk:
                    t_blk[g] = tpool.tile([P, 2, 3, GT, HD], F32, name="tt")
                v_blk[g] = tpool.tile([P, GT, HD], F32, name="vo")
            return passes(g, hb)

        def products(g, hb, y, ta, tz):
            n, gi = divmod(g, GPB)
            t0 = gi * GT
            nc.vector.tensor_tensor(
                out=t_blk[g][:, :, hb, ta:tz, :].rearrange("p r t d -> p r (t d)"),
                in0=y[:, ta * HD : tz * HD].unsqueeze(1).to_broadcast([P, 2, (tz - ta) * HD]),
                in1=cs_blk[n][:, :, t0 + ta : t0 + tz, :].rearrange("p r t d -> p r (t d)"),
                op=ALU.mult,
            )

        def head(g, hb):
            if g in TURNED and hb < 3:
                turned_head(g, hb)
                return
            y = multiply(g, hb)
            if hb < 3:
                products(g, hb, y, 0, GT)
            else:
                nc.scalar.copy(out=v_blk[g][:].rearrange("p t d -> p (t d)"), in_=y[:])

        ww = w_sb[:].bitcast(F32)
        wgw = wgrp[:].bitcast(F32)
        new_block(0)
        nc.sync.dma_start(
            out=w_sb[:, 0 : 2 * H].rearrange("p (a k) -> p a k", a=2), in_=q_w.rearrange("(a p) k -> p a k", p=P)
        )
        load_x(0, 0, 2)
        load_x(0, 2, 4)
        load_sin(0)
        nc.sync.dma_start(out=w_sb[:, 2 * H : 3 * H], in_=k_w)
        nc.sync.dma_start(out=w_sb[:, 3 * H : 4 * H], in_=v_w)
        load_cos(0)
        load_x(0, 4, 8)
        new_block(1)
        load_x(1, 0, 4)
        load_x(1, 4, 8)
        load_sin(1)
        load_cos(1)
        for n in range(2, XBUFS):
            load_block(n)

        transpose_pair(ww[:, 0:512], wgw[:, 0:512], True, early=True)
        prep_half(0, 0)
        prep_half(0, 1)
        transpose_pair(ww[:, 512:1024], wgw[:, 512:1024], False, early=True)
        new_codes(0)
        quantise(wgrp, wc, ws, 0, 256)
        quantise(grp_of[0], q_of[0][0], q_of[0][1], 0, 256)
        nc.vector.tensor_copy(out=cs_blk[0][:, 1, :, 0:64], in_=sn_blk[0][:, :, 64:128])
        quantise(grp_of[0], q_of[0][0], q_of[0][1], 256, 512)
        nc.vector.tensor_scalar_mul(out=cs_blk[0][:, 1, :, 64:128], in0=sn_blk[0][:, :, 0:64], scalar1=-1.0)

        BACKS = {(1,1): 0,(1,2): 1,(2,1): 2}

        def back(g, pos):
            for d in (1, 2):
                if g - d in TURNED and (d, pos) in BACKS:
                    h = BACKS[d, pos]
                    turn_back(g - d, h)
                    store(g - d, ("q0", "q1", "k")[h])

        turned = [2]

        def turn_x(g):
            while turned[-1] < g:
                turned.append(turned[-1] + 1)
                prep(turned[-1])

        for g in range(NG - 1):
            n, gi = divmod(g, GPB)
            if g >= V_FIRST:
                head(g, 3)
                store(g, "v")
                if g - 1 not in TURNED:
                    store(g - 1, "q")
                    store(g - 1, "k")
            head(g, 0)
            if g == 0:
                quantise(wgrp, wc, ws, 256, 512)
            back(g, 0)
            head(g, 1)
            back(g, 1)
            if g == 0:
                prep(1)
                quant(1)
            if g == 0:
                y = multiply(g, 2)
                prep(g + 2)
                head(g, 3)
                products(g, 2, y, 0, GT - 1)
                quant(g + 2)
                products(g, 2, y, GT - 1, GT)
            else:
                head(g, 2)
                back(g, 2)
                if g < V_FIRST:
                    head(g, 3)
                back(g, 3)
                turn_x(min(g + min(g + 1, LEAD), NG - 1))
                if g + 2 < NG and chunk(g + 2)[0] == g + 2:
                    quant(g + 2)
            if gi == 0 and n + 1 < NBLK:
                swap_sin(n + 1, False)
            if g + 2 in TURNED:
                turn_tables(g + 2)
            if g == 13:
                turn_tables(NG - 1)
            if g in TURNED:
                pass
            elif g < NG - 3:
                combine(nc.gpsimd, g, 0, 3)
            else:
                combine(nc.gpsimd, g, 0, 2)
                combine(nc.gpsimd, g, 2, 3)
            if g < V_FIRST - 1 and g not in TURNED:
                for what in ("v", "q", "k"):
                    store(g, what)
            elif g < V_FIRST:
                store(g, "v")
            if gi == GPB - 1 and n + XBUFS < NBLK:
                load_block(n + XBUFS)

        g = NG - 1
        head(g, 3)
        store(g, "v")
        store(g - 1, "q")
        store(g - 1, "k")
        turned_head(g, 2)
        head(g, 0)
        head(g, 1)
        back(g, 1)
        turn_back(g, 2)
        store(g, "k")
        combine(nc.vector, g, 0, 1)
        store(g, "q0")
        combine(nc.vector, g, 1, 2)
        store(g, "q1")
